import numpy as np
import ml_dtypes

BF16 = ml_dtypes.bfloat16


def bf(x):
    return np.asarray(x, np.float32).astype(BF16)


def f32(x):
    return np.asarray(x, np.float32)


def f64(x):
    return np.asarray(x).astype(np.float64)


def striped(idx):
    return np.tile(idx.reshape(-1, 16).T, (8, 1))


V, D, Q, N = 4096, 128, 512, 1024


def setup_inputs():
    return {"table": bf(np.random.standard_normal((D, V))), "w": bf(np.random.standard_normal((D, Q)) / np.sqrt(D)), "fc2": bf(np.random.standard_normal((Q, D)) / np.sqrt(Q)), "offs": striped(np.random.permutation(np.tile(np.arange(V), 2))[:N])}


def reference(table, w, fc2, offs):
    idx = offs[:16].T.reshape(-1)
    h = np.square(np.maximum(f64(w).T @ f64(table)[:, idx], 0.0))
    return f64(fc2).T @ h

@@ -1,0 +1,57 @@
+import concourse.mybir as mybir
+
+BF16, F32, U16 = mybir.dt.bfloat16, mybir.dt.float32, mybir.dt.uint16
+RELU = mybir.ActivationFunctionType.Relu
+MULT = mybir.AluOpType.mult
+
+P = 128
+V = 4096
+Q = 512
+N = 1024
+PIECE = 512
+Q_BLOCKS = Q // P
+PIECES = N // PIECE
+OFFSET_COLUMNS = PIECE // 16
+
+FLOPS = 2 * P * Q * N + 2 * Q * P * N
+
+
+def tile_gptmodel_kernel(tc, table, w, fc2, offs, out):
+    nc = tc.nc
+    with (
+        tc.tile_pool(name="held", bufs=1) as held,
+        tc.tile_pool(name="work", bufs=4) as work,
+        tc.tile_pool(name="hidden", bufs=PIECES * Q_BLOCKS) as hidden,
+        tc.psum_pool(name="hidden_psum", bufs=6) as hidden_psum,
+        tc.psum_pool(name="out_psum", bufs=2) as out_psum,
+    ):
+        offsets = held.tile([P, N // 16], U16, name="offsets")
+        nc.sync.dma_start(offsets[:], offs)
+        table_sb = held.tile([P, V], BF16, name="table_sb")
+        nc.sync.dma_start(table_sb[:], table)
+        w_sb = held.tile([P, Q], BF16, name="w_sb")
+        nc.scalar.dma_start(w_sb[:], w)
+        fc2_sb = held.tile([P, Q_BLOCKS, P], BF16, name="fc2_sb")
+        nc.scalar.dma_start(fc2_sb[:], fc2.rearrange("(b p) d -> p b d", p=P))
+
+        h_tiles = {}
+        for piece in range(PIECES):
+            piece_offsets = offsets[:, piece * OFFSET_COLUMNS : (piece + 1) * OFFSET_COLUMNS]
+            for b in range(Q_BLOCKS):
+                x = hidden_psum.tile([P, PIECE], F32, name="x")
+                nc.tensor.matmul(
+                    x[:], w_sb[:, b * P : (b + 1) * P], table_sb[:].indirect(piece_offsets), start=True, stop=True
+                )
+                r = work.tile([P, PIECE], F32, name="r")
+                nc.scalar.activation(r[:], x[:], RELU)
+                h = hidden.tile([P, PIECE], BF16, name="h")
+                nc.vector.tensor_tensor(h[:], r[:], r[:], MULT)
+                h_tiles[piece, b] = h
+
+        for piece in range(PIECES):
+            y = out_psum.tile([P, PIECE], F32, name="y")
+            for b in range(Q_BLOCKS):
+                nc.tensor.matmul(y[:], fc2_sb[:, b, :], h_tiles[piece, b][:], start=(b == 0), stop=(b == Q_BLOCKS - 1))
+            y_sb = work.tile([P, PIECE], F32, name="y_sb")
+            nc.vector.tensor_copy(y_sb[:], y[:])
+            nc.sync.dma_start(out[:, piece * PIECE : (piece + 1) * PIECE], y_sb[:])

@@ -13,6 +13,8 @@ Q_BLOCKS = Q // P
 PIECES = N // PIECE
 OFFSET_COLUMNS = PIECE // 16
 
+WARM_UP = 6
+
 FLOPS = 2 * P * Q * N + 2 * Q * P * N
 
 
@@ -33,6 +35,10 @@ def tile_gptmodel_kernel(tc, table, w, fc2, offs, out):
         nc.scalar.dma_start(w_sb[:], w)
         fc2_sb = held.tile([P, Q_BLOCKS, P], BF16, name="fc2_sb")
         nc.scalar.dma_start(fc2_sb[:], fc2.rearrange("(b p) d -> p b d", p=P))
+
+        warm = hidden_psum.tile([P, Q], F32, name="warm", tag="x")
+        for i in range(WARM_UP):
+            nc.tensor.matmul(warm[:], w_sb[:, 0:P], w_sb[:], start=True, stop=True)
 
         h_tiles = {}
         for piece in range(PIECES):

@@ -13,8 +13,6 @@ Q_BLOCKS = Q // P
 PIECES = N // PIECE
 OFFSET_COLUMNS = PIECE // 16
 
-WARM_UP = 6
-
 FLOPS = 2 * P * Q * N + 2 * Q * P * N
 
 
@@ -36,10 +34,6 @@ def tile_gptmodel_kernel(tc, table, w, fc2, offs, out):
         fc2_sb = held.tile([P, Q_BLOCKS, P], BF16, name="fc2_sb")
         nc.scalar.dma_start(fc2_sb[:], fc2.rearrange("(b p) d -> p b d", p=P))
 
-        warm = hidden_psum.tile([P, Q], F32, name="warm", tag="x")
-        for i in range(WARM_UP):
-            nc.tensor.matmul(warm[:], w_sb[:, 0:P], w_sb[:], start=True, stop=True)
-
         h_tiles = {}
         for piece in range(PIECES):
             piece_offsets = offsets[:, piece * OFFSET_COLUMNS : (piece + 1) * OFFSET_COLUMNS]
@@ -59,5 +53,8 @@ def tile_gptmodel_kernel(tc, table, w, fc2, offs, out):
             for b in range(Q_BLOCKS):
                 nc.tensor.matmul(y[:], fc2_sb[:, b, :], h_tiles[piece, b][:], start=(b == 0), stop=(b == Q_BLOCKS - 1))
             y_sb = work.tile([P, PIECE], F32, name="y_sb")
-            nc.vector.tensor_copy(y_sb[:], y[:])
+            if piece < PIECES - 1:
+                nc.scalar.copy(y_sb[:], y[:])
+            else:
+                nc.vector.tensor_copy(y_sb[:], y[:])
             nc.sync.dma_start(out[:, piece * PIECE : (piece + 1) * PIECE], y_sb[:])

@@ -13,6 +13,9 @@ Q_BLOCKS = Q // P
 PIECES = N // PIECE
 OFFSET_COLUMNS = PIECE // 16
 
+TABLE_CHUNKS = 4
+CHUNK = V // TABLE_CHUNKS
+
 FLOPS = 2 * P * Q * N + 2 * Q * P * N
 
 
@@ -28,11 +31,18 @@ def tile_gptmodel_kernel(tc, table, w, fc2, offs, out):
         offsets = held.tile([P, N // 16], U16, name="offsets")
         nc.sync.dma_start(offsets[:], offs)
         table_sb = held.tile([P, V], BF16, name="table_sb")
-        nc.sync.dma_start(table_sb[:], table)
+        for c in range(TABLE_CHUNKS):
+            nc.sync.dma_start(table_sb[:, c * CHUNK : (c + 1) * CHUNK], table[:, c * CHUNK : (c + 1) * CHUNK])
         w_sb = held.tile([P, Q], BF16, name="w_sb")
         nc.scalar.dma_start(w_sb[:], w)
         fc2_sb = held.tile([P, Q_BLOCKS, P], BF16, name="fc2_sb")
         nc.scalar.dma_start(fc2_sb[:], fc2.rearrange("(b p) d -> p b d", p=P))
+
+        warm = hidden_psum.tile([P, PIECE], F32, name="warm", tag="x")
+        for first_column in range(0, (TABLE_CHUNKS - 1) * CHUNK, PIECE):
+            nc.tensor.matmul(
+                warm[:], w_sb[:, 0:P], table_sb[:, first_column : first_column + PIECE], start=True, stop=True
+            )
 
         h_tiles = {}
         for piece in range(PIECES):

@@ -13,9 +13,6 @@ Q_BLOCKS = Q // P
 PIECES = N // PIECE
 OFFSET_COLUMNS = PIECE // 16
 
-TABLE_CHUNKS = 4
-CHUNK = V // TABLE_CHUNKS
-
 FLOPS = 2 * P * Q * N + 2 * Q * P * N
 
 
@@ -30,19 +27,12 @@ def tile_gptmodel_kernel(tc, table, w, fc2, offs, out):
     ):
         offsets = held.tile([P, N // 16], U16, name="offsets")
         nc.sync.dma_start(offsets[:], offs)
-        table_sb = held.tile([P, V], BF16, name="table_sb")
-        for c in range(TABLE_CHUNKS):
-            nc.sync.dma_start(table_sb[:, c * CHUNK : (c + 1) * CHUNK], table[:, c * CHUNK : (c + 1) * CHUNK])
         w_sb = held.tile([P, Q], BF16, name="w_sb")
-        nc.scalar.dma_start(w_sb[:], w)
+        nc.sync.dma_start(w_sb[:], w)
+        table_sb = held.tile([P, V], BF16, name="table_sb")
+        nc.sync.dma_start(table_sb[:], table)
         fc2_sb = held.tile([P, Q_BLOCKS, P], BF16, name="fc2_sb")
-        nc.scalar.dma_start(fc2_sb[:], fc2.rearrange("(b p) d -> p b d", p=P))
-
-        warm = hidden_psum.tile([P, PIECE], F32, name="warm", tag="x")
-        for first_column in range(0, (TABLE_CHUNKS - 1) * CHUNK, PIECE):
-            nc.tensor.matmul(
-                warm[:], w_sb[:, 0:P], table_sb[:, first_column : first_column + PIECE], start=True, stop=True
-            )
+        nc.sync.dma_start(fc2_sb[:], fc2.rearrange("(b p) d -> p b d", p=P))
 
         h_tiles = {}
         for piece in range(PIECES):

@@ -9,6 +9,7 @@ V = 4096
 Q = 512
 N = 1024
 PIECE = 512
+HALF = PIECE // 2
 Q_BLOCKS = Q // P
 PIECES = N // PIECE
 OFFSET_COLUMNS = PIECE // 16
@@ -52,9 +53,11 @@ def tile_gptmodel_kernel(tc, table, w, fc2, offs, out):
             y = out_psum.tile([P, PIECE], F32, name="y")
             for b in range(Q_BLOCKS):
                 nc.tensor.matmul(y[:], fc2_sb[:, b, :], h_tiles[piece, b][:], start=(b == 0), stop=(b == Q_BLOCKS - 1))
-            y_sb = work.tile([P, PIECE], F32, name="y_sb")
-            if piece < PIECES - 1:
-                nc.scalar.copy(y_sb[:], y[:])
-            else:
-                nc.vector.tensor_copy(y_sb[:], y[:])
-            nc.sync.dma_start(out[:, piece * PIECE : (piece + 1) * PIECE], y_sb[:])
+            for half, queue in enumerate((nc.sync, nc.scalar)):
+                y_sb = work.tile([P, HALF], F32, name="y_sb")
+                if piece < PIECES - 1:
+                    nc.scalar.copy(y_sb[:], y[:, half * HALF : (half + 1) * HALF])
+                else:
+                    nc.vector.tensor_copy(y_sb[:], y[:, half * HALF : (half + 1) * HALF])
+                first_column = piece * PIECE + half * HALF
+                queue.dma_start(out[:, first_column : first_column + HALF], y_sb[:])

@@ -8,11 +8,9 @@ P = 128
 V = 4096
 Q = 512
 N = 1024
-PIECE = 512
-HALF = PIECE // 2
 Q_BLOCKS = Q // P
-PIECES = N // PIECE
-OFFSET_COLUMNS = PIECE // 16
+PSUM_BANKS = 8
+PIECES = ((0, 256), (256, 512), (768, 256))
 
 FLOPS = 2 * P * Q * N + 2 * Q * P * N
 
@@ -22,9 +20,8 @@ def tile_gptmodel_kernel(tc, table, w, fc2, offs, out):
     with (
         tc.tile_pool(name="held", bufs=1) as held,
         tc.tile_pool(name="work", bufs=4) as work,
-        tc.tile_pool(name="hidden", bufs=PIECES * Q_BLOCKS) as hidden,
-        tc.psum_pool(name="hidden_psum", bufs=6) as hidden_psum,
-        tc.psum_pool(name="out_psum", bufs=2) as out_psum,
+        tc.tile_pool(name="hidden", bufs=len(PIECES) * Q_BLOCKS) as hidden,
+        tc.psum_pool(name="psum", bufs=PSUM_BANKS) as psum,
     ):
         offsets = held.tile([P, N // 16], U16, name="offsets")
         nc.sync.dma_start(offsets[:], offs)
@@ -36,28 +33,26 @@ def tile_gptmodel_kernel(tc, table, w, fc2, offs, out):
         nc.sync.dma_start(fc2_sb[:], fc2.rearrange("(b p) d -> p b d", p=P))
 
         h_tiles = {}
-        for piece in range(PIECES):
-            piece_offsets = offsets[:, piece * OFFSET_COLUMNS : (piece + 1) * OFFSET_COLUMNS]
+        for first, width in PIECES:
+            piece_offsets = offsets[:, first // 16 : (first + width) // 16]
             for b in range(Q_BLOCKS):
-                x = hidden_psum.tile([P, PIECE], F32, name="x")
+                x = psum.tile([P, width], F32, name="x", tag="bank")
                 nc.tensor.matmul(
                     x[:], w_sb[:, b * P : (b + 1) * P], table_sb[:].indirect(piece_offsets), start=True, stop=True
                 )
-                r = work.tile([P, PIECE], F32, name="r")
+                r = work.tile([P, width], F32, name="r")
                 nc.scalar.activation(r[:], x[:], RELU)
-                h = hidden.tile([P, PIECE], BF16, name="h")
+                h = hidden.tile([P, width], BF16, name="h")
                 nc.vector.tensor_tensor(h[:], r[:], r[:], MULT)
-                h_tiles[piece, b] = h
+                h_tiles[first, b] = h
 
-        for piece in range(PIECES):
-            y = out_psum.tile([P, PIECE], F32, name="y")
+        for first, width in PIECES:
+            y = psum.tile([P, width], F32, name="y", tag="bank")
             for b in range(Q_BLOCKS):
-                nc.tensor.matmul(y[:], fc2_sb[:, b, :], h_tiles[piece, b][:], start=(b == 0), stop=(b == Q_BLOCKS - 1))
-            for half, queue in enumerate((nc.sync, nc.scalar)):
-                y_sb = work.tile([P, HALF], F32, name="y_sb")
-                if piece < PIECES - 1:
-                    nc.scalar.copy(y_sb[:], y[:, half * HALF : (half + 1) * HALF])
-                else:
-                    nc.vector.tensor_copy(y_sb[:], y[:, half * HALF : (half + 1) * HALF])
-                first_column = piece * PIECE + half * HALF
-                queue.dma_start(out[:, first_column : first_column + HALF], y_sb[:])
+                nc.tensor.matmul(y[:], fc2_sb[:, b, :], h_tiles[first, b][:], start=(b == 0), stop=(b == Q_BLOCKS - 1))
+            y_sb = work.tile([P, width], F32, name="y_sb")
+            if first + width < N:
+                nc.scalar.copy(y_sb[:], y[:])
+            else:
+                nc.vector.tensor_copy(y_sb[:], y[:])
+            nc.sync.dma_start(out[:, first : first + width], y_sb[:])

@@ -8,9 +8,11 @@ P = 128
 V = 4096
 Q = 512
 N = 1024
+PIECE = 512
 Q_BLOCKS = Q // P
 PSUM_BANKS = 8
-PIECES = ((0, 256), (256, 512), (768, 256))
+PIECES = N // PIECE
+OFFSET_COLUMNS = PIECE // 16
 
 FLOPS = 2 * P * Q * N + 2 * Q * P * N
 
@@ -20,7 +22,7 @@ def tile_gptmodel_kernel(tc, table, w, fc2, offs, out):
     with (
         tc.tile_pool(name="held", bufs=1) as held,
         tc.tile_pool(name="work", bufs=4) as work,
-        tc.tile_pool(name="hidden", bufs=len(PIECES) * Q_BLOCKS) as hidden,
+        tc.tile_pool(name="hidden", bufs=PIECES * Q_BLOCKS) as hidden,
         tc.psum_pool(name="psum", bufs=PSUM_BANKS) as psum,
     ):
         offsets = held.tile([P, N // 16], U16, name="offsets")
@@ -33,26 +35,38 @@ def tile_gptmodel_kernel(tc, table, w, fc2, offs, out):
         nc.sync.dma_start(fc2_sb[:], fc2.rearrange("(b p) d -> p b d", p=P))
 
         h_tiles = {}
-        for first, width in PIECES:
-            piece_offsets = offsets[:, first // 16 : (first + width) // 16]
+        for piece in range(PIECES):
+            piece_offsets = offsets[:, piece * OFFSET_COLUMNS : (piece + 1) * OFFSET_COLUMNS]
             for b in range(Q_BLOCKS):
-                x = psum.tile([P, width], F32, name="x", tag="bank")
+                x = psum.tile([P, PIECE], F32, name="x", tag="bank")
                 nc.tensor.matmul(
                     x[:], w_sb[:, b * P : (b + 1) * P], table_sb[:].indirect(piece_offsets), start=True, stop=True
                 )
-                r = work.tile([P, width], F32, name="r")
+                r = work.tile([P, PIECE], F32, name="r")
                 nc.scalar.activation(r[:], x[:], RELU)
-                h = hidden.tile([P, width], BF16, name="h")
+                h = hidden.tile([P, PIECE], BF16, name="h")
                 nc.vector.tensor_tensor(h[:], r[:], r[:], MULT)
-                h_tiles[first, b] = h
+                h_tiles[piece, b] = h
 
-        for first, width in PIECES:
-            y = psum.tile([P, width], F32, name="y", tag="bank")
+        for piece in range(PIECES):
+            parts = 2 if piece == PIECES - 1 else 1
+            width = PIECE // parts
+            y_parts = [psum.tile([P, width], F32, name="y", tag="bank") for part in range(parts)]
             for b in range(Q_BLOCKS):
-                nc.tensor.matmul(y[:], fc2_sb[:, b, :], h_tiles[first, b][:], start=(b == 0), stop=(b == Q_BLOCKS - 1))
-            y_sb = work.tile([P, width], F32, name="y_sb")
-            if first + width < N:
-                nc.scalar.copy(y_sb[:], y[:])
-            else:
-                nc.vector.tensor_copy(y_sb[:], y[:])
-            nc.sync.dma_start(out[:, first : first + width], y_sb[:])
+                for part in range(parts):
+                    nc.tensor.matmul(
+                        y_parts[part][:],
+                        fc2_sb[:, b, :],
+                        h_tiles[piece, b][:, part * width : (part + 1) * width],
+                        start=(b == 0),
+                        stop=(b == Q_BLOCKS - 1),
+                    )
+            for part in range(parts):
+                first_column = piece * PIECE + part * width
+                y_sb = work.tile([P, width], F32, name="y_sb")
+                if part == 0:
+                    nc.scalar.copy(y_sb[:], y_parts[part][:])
+                    nc.scalar.dma_start(out[:, first_column : first_column + width], y_sb[:])
+                else:
+                    nc.vector.tensor_copy(y_sb[:], y_parts[part][:])
+                    nc.sync.dma_start(out[:, first_column : first_column + width], y_sb[:])

@@ -27,10 +27,13 @@ def tile_gptmodel_kernel(tc, table, w, fc2, offs, out):
     ):
         offsets = held.tile([P, N // 16], U16, name="offsets")
         nc.sync.dma_start(offsets[:], offs)
-        w_sb = held.tile([P, Q], BF16, name="w_sb")
-        nc.sync.dma_start(w_sb[:], w)
+        w_first = held.tile([P, P], BF16, name="w_first")
+        nc.sync.dma_start(w_first[:], w[:, 0:P])
         table_sb = held.tile([P, V], BF16, name="table_sb")
         nc.sync.dma_start(table_sb[:], table)
+        w_rest = held.tile([P, Q - P], BF16, name="w_rest")
+        nc.sync.dma_start(w_rest[:], w[:, P:Q])
+        w_blocks = [w_first[:]] + [w_rest[:, (b - 1) * P : b * P] for b in range(1, Q_BLOCKS)]
         fc2_sb = held.tile([P, Q_BLOCKS, P], BF16, name="fc2_sb")
         nc.sync.dma_start(fc2_sb[:], fc2.rearrange("(b p) d -> p b d", p=P))
 
@@ -40,7 +43,7 @@ def tile_gptmodel_kernel(tc, table, w, fc2, offs, out):
             for b in range(Q_BLOCKS):
                 x = psum.tile([P, PIECE], F32, name="x", tag="bank")
                 nc.tensor.matmul(
-                    x[:], w_sb[:, b * P : (b + 1) * P], table_sb[:].indirect(piece_offsets), start=True, stop=True
+                    x[:], w_blocks[b], table_sb[:].indirect(piece_offsets), start=True, stop=True
                 )
                 r = work.tile([P, PIECE], F32, name="r")
                 nc.scalar.activation(r[:], x[:], RELU)

@@ -69,7 +69,6 @@ def tile_gptmodel_kernel(tc, table, w, fc2, offs, out):
                 y_sb = work.tile([P, width], F32, name="y_sb")
                 if part == 0:
                     nc.scalar.copy(y_sb[:], y_parts[part][:])
-                    nc.scalar.dma_start(out[:, first_column : first_column + width], y_sb[:])
                 else:
                     nc.vector.tensor_copy(y_sb[:], y_parts[part][:])
-                    nc.sync.dma_start(out[:, first_column : first_column + width], y_sb[:])
+                nc.sync.dma_start(out[:, first_column : first_column + width], y_sb[:])

@@ -25,12 +25,12 @@ def tile_gptmodel_kernel(tc, table, w, fc2, offs, out):
         tc.tile_pool(name="hidden", bufs=PIECES * Q_BLOCKS) as hidden,
         tc.psum_pool(name="psum", bufs=PSUM_BANKS) as psum,
     ):
+        table_sb = held.tile([P, V], BF16, name="table_sb")
+        nc.sync.dma_start(table_sb[:], table)
         offsets = held.tile([P, N // 16], U16, name="offsets")
         nc.sync.dma_start(offsets[:], offs)
         w_first = held.tile([P, P], BF16, name="w_first")
         nc.sync.dma_start(w_first[:], w[:, 0:P])
-        table_sb = held.tile([P, V], BF16, name="table_sb")
-        nc.sync.dma_start(table_sb[:], table)
         w_rest = held.tile([P, Q - P], BF16, name="w_rest")
         nc.sync.dma_start(w_rest[:], w[:, P:Q])
         w_blocks = [w_first[:]] + [w_rest[:, (b - 1) * P : b * P] for b in range(1, Q_BLOCKS)]

@@ -1,7 +1,7 @@
 import concourse.mybir as mybir
 
 BF16, F32, U16 = mybir.dt.bfloat16, mybir.dt.float32, mybir.dt.uint16
-RELU = mybir.ActivationFunctionType.Relu
+RELU, SQUARE = mybir.ActivationFunctionType.Relu, mybir.ActivationFunctionType.Square
 MULT = mybir.AluOpType.mult
 
 P = 128
@@ -12,7 +12,7 @@ PIECE = 512
 Q_BLOCKS = Q // P
 PSUM_BANKS = 8
 PIECES = N // PIECE
-OFFSET_COLUMNS = PIECE // 16
+HALF = PIECE // 2
 
 FLOPS = 2 * P * Q * N + 2 * Q * P * N
 
@@ -22,7 +22,7 @@ def tile_gptmodel_kernel(tc, table, w, fc2, offs, out):
     with (
         tc.tile_pool(name="held", bufs=1) as held,
         tc.tile_pool(name="work", bufs=4) as work,
-        tc.tile_pool(name="hidden", bufs=PIECES * Q_BLOCKS) as hidden,
+        tc.tile_pool(name="hidden", bufs=PIECES * Q_BLOCKS + 1) as hidden,
         tc.psum_pool(name="psum", bufs=PSUM_BANKS) as psum,
     ):
         table_sb = held.tile([P, V], BF16, name="table_sb")
@@ -37,38 +37,44 @@ def tile_gptmodel_kernel(tc, table, w, fc2, offs, out):
         fc2_sb = held.tile([P, Q_BLOCKS, P], BF16, name="fc2_sb")
         nc.sync.dma_start(fc2_sb[:], fc2.rearrange("(b p) d -> p b d", p=P))
 
-        h_tiles = {}
+        h_columns = {b: [] for b in range(Q_BLOCKS)}
         for piece in range(PIECES):
-            piece_offsets = offsets[:, piece * OFFSET_COLUMNS : (piece + 1) * OFFSET_COLUMNS]
             for b in range(Q_BLOCKS):
-                x = psum.tile([P, PIECE], F32, name="x", tag="bank")
-                nc.tensor.matmul(
-                    x[:], w_blocks[b], table_sb[:].indirect(piece_offsets), start=True, stop=True
-                )
-                r = work.tile([P, PIECE], F32, name="r")
-                nc.scalar.activation(r[:], x[:], RELU)
-                h = hidden.tile([P, PIECE], BF16, name="h")
-                nc.vector.tensor_tensor(h[:], r[:], r[:], MULT)
-                h_tiles[piece, b] = h
-
-        for piece in range(PIECES):
-            parts = 2 if piece == PIECES - 1 else 1
-            width = PIECE // parts
-            y_parts = [psum.tile([P, width], F32, name="y", tag="bank") for part in range(parts)]
-            for b in range(Q_BLOCKS):
+                parts = 2 if (piece, b) == (PIECES - 1, Q_BLOCKS - 1) else 1
+                width = PIECE // parts
+                r_parts = []
                 for part in range(parts):
-                    nc.tensor.matmul(
-                        y_parts[part][:],
-                        fc2_sb[:, b, :],
-                        h_tiles[piece, b][:, part * width : (part + 1) * width],
-                        start=(b == 0),
-                        stop=(b == Q_BLOCKS - 1),
-                    )
-            for part in range(parts):
-                first_column = piece * PIECE + part * width
-                y_sb = work.tile([P, width], F32, name="y_sb")
-                if part == 0:
-                    nc.scalar.copy(y_sb[:], y_parts[part][:])
-                else:
-                    nc.vector.tensor_copy(y_sb[:], y_parts[part][:])
-                nc.sync.dma_start(out[:, first_column : first_column + width], y_sb[:])
+                    first_id = piece * PIECE + part * width
+                    ids = offsets[:, first_id // 16 : (first_id + width) // 16]
+                    x = psum.tile([P, width], F32, name="x", tag="bank")
+                    nc.tensor.matmul(x[:], w_blocks[b], table_sb[:].indirect(ids), start=True, stop=True)
+                    r = work.tile([P, width], F32, name="r")
+                    nc.scalar.activation(r[:], x[:], RELU)
+                    r_parts.append(r)
+                for part in range(parts):
+                    r = r_parts[part]
+                    h = hidden.tile([P, width], BF16, name="h")
+                    if part < parts - 1:
+                        nc.scalar.activation(h[:], r[:], SQUARE)
+                    else:
+                        nc.vector.tensor_tensor(h[:], r[:], r[:], MULT)
+                    h_columns[b].append((piece * PIECE + part * width, width, h))
+
+        for run, (first, last) in enumerate(((0, PIECE), (PIECE, PIECE + HALF), (PIECE + HALF, N))):
+            y = psum.tile([P, last - first], F32, name="y", tag="bank")
+            for b in range(Q_BLOCKS):
+                for first_id, width, h in h_columns[b]:
+                    if first_id <= first and last <= first_id + width:
+                        nc.tensor.matmul(
+                            y[:],
+                            fc2_sb[:, b, :],
+                            h[:, first - first_id : last - first_id],
+                            start=(b == 0),
+                            stop=(b == Q_BLOCKS - 1),
+                        )
+            y_sb = work.tile([P, last - first], F32, name="y_sb")
+            if run % 2 == 0:
+                nc.scalar.copy(y_sb[:], y[:])
+            else:
+                nc.vector.tensor_copy(y_sb[:], y[:])
+            nc.sync.dma_start(out[:, first:last], y_sb[:])

@@ -12,7 +12,7 @@ PIECE = 512
 Q_BLOCKS = Q // P
 PSUM_BANKS = 8
 PIECES = N // PIECE
-HALF = PIECE // 2
+STORES = ((0, 512, (384, 128)), (512, 768, (256,)), (768, 1024, (128, 128)))
 
 FLOPS = 2 * P * Q * N + 2 * Q * P * N
 
@@ -22,7 +22,7 @@ def tile_gptmodel_kernel(tc, table, w, fc2, offs, out):
     with (
         tc.tile_pool(name="held", bufs=1) as held,
         tc.tile_pool(name="work", bufs=4) as work,
-        tc.tile_pool(name="hidden", bufs=PIECES * Q_BLOCKS + 1) as hidden,
+        tc.tile_pool(name="hidden", bufs=PIECES * Q_BLOCKS) as hidden,
         tc.psum_pool(name="psum", bufs=PSUM_BANKS) as psum,
     ):
         table_sb = held.tile([P, V], BF16, name="table_sb")
@@ -37,11 +37,12 @@ def tile_gptmodel_kernel(tc, table, w, fc2, offs, out):
         fc2_sb = held.tile([P, Q_BLOCKS, P], BF16, name="fc2_sb")
         nc.sync.dma_start(fc2_sb[:], fc2.rearrange("(b p) d -> p b d", p=P))
 
-        h_columns = {b: [] for b in range(Q_BLOCKS)}
+        h_tiles = {}
         for piece in range(PIECES):
             for b in range(Q_BLOCKS):
                 parts = 2 if (piece, b) == (PIECES - 1, Q_BLOCKS - 1) else 1
                 width = PIECE // parts
+                h = hidden.tile([P, PIECE], BF16, name="h")
                 r_parts = []
                 for part in range(parts):
                     first_id = piece * PIECE + part * width
@@ -52,29 +53,32 @@ def tile_gptmodel_kernel(tc, table, w, fc2, offs, out):
                     nc.scalar.activation(r[:], x[:], RELU)
                     r_parts.append(r)
                 for part in range(parts):
-                    r = r_parts[part]
-                    h = hidden.tile([P, width], BF16, name="h")
+                    r, h_part = r_parts[part], h[:, part * width : (part + 1) * width]
                     if part < parts - 1:
-                        nc.scalar.activation(h[:], r[:], SQUARE)
+                        nc.scalar.activation(h_part, r[:], SQUARE)
                     else:
-                        nc.vector.tensor_tensor(h[:], r[:], r[:], MULT)
-                    h_columns[b].append((piece * PIECE + part * width, width, h))
+                        nc.vector.tensor_tensor(h_part, r[:], r[:], MULT)
+                h_tiles[piece, b] = h
 
-        for run, (first, last) in enumerate(((0, PIECE), (PIECE, PIECE + HALF), (PIECE + HALF, N))):
-            y = psum.tile([P, last - first], F32, name="y", tag="bank")
-            for b in range(Q_BLOCKS):
-                for first_id, width, h in h_columns[b]:
-                    if first_id <= first and last <= first_id + width:
-                        nc.tensor.matmul(
-                            y[:],
-                            fc2_sb[:, b, :],
-                            h[:, first - first_id : last - first_id],
-                            start=(b == 0),
-                            stop=(b == Q_BLOCKS - 1),
-                        )
-            y_sb = work.tile([P, last - first], F32, name="y_sb")
-            if run % 2 == 0:
-                nc.scalar.copy(y_sb[:], y[:])
-            else:
-                nc.vector.tensor_copy(y_sb[:], y[:])
-            nc.sync.dma_start(out[:, first:last], y_sb[:])
+        for store_first, store_last, widths in STORES:
+            y_sb = work.tile([P, store_last - store_first], F32, name="y_sb")
+            first = store_first
+            for width in widths:
+                piece, column = first // PIECE, first % PIECE
+                y = psum.tile([P, width], F32, name="y", tag="bank")
+                blocks = list(range(Q_BLOCKS)) if column == 0 else [Q_BLOCKS - 1] + list(range(Q_BLOCKS - 1))
+                for b in blocks:
+                    nc.tensor.matmul(
+                        y[:],
+                        fc2_sb[:, b, :],
+                        h_tiles[piece, b][:, column : column + width],
+                        start=(b == blocks[0]),
+                        stop=(b == blocks[-1]),
+                    )
+                copied = y_sb[:, first - store_first : first - store_first + width]
+                if piece == 0 or first + width == N:
+                    nc.scalar.copy(copied, y[:])
+                else:
+                    nc.vector.tensor_copy(copied, y[:])
+                first += width
+            nc.sync.dma_start(out[:, store_first:store_last], y_sb[:])

@@ -2,7 +2,7 @@ import concourse.mybir as mybir
 
 BF16, F32, U16 = mybir.dt.bfloat16, mybir.dt.float32, mybir.dt.uint16
 RELU, SQUARE = mybir.ActivationFunctionType.Relu, mybir.ActivationFunctionType.Square
-MULT = mybir.AluOpType.mult
+MAX, MULT = mybir.AluOpType.max, mybir.AluOpType.mult
 
 P = 128
 V = 4096
@@ -43,21 +43,24 @@ def tile_gptmodel_kernel(tc, table, w, fc2, offs, out):
                 parts = 2 if (piece, b) == (PIECES - 1, Q_BLOCKS - 1) else 1
                 width = PIECE // parts
                 h = hidden.tile([P, PIECE], BF16, name="h")
-                r_parts = []
+                moved = []
                 for part in range(parts):
                     first_id = piece * PIECE + part * width
                     ids = offsets[:, first_id // 16 : (first_id + width) // 16]
                     x = psum.tile([P, width], F32, name="x", tag="bank")
                     nc.tensor.matmul(x[:], w_blocks[b], table_sb[:].indirect(ids), start=True, stop=True)
-                    r = work.tile([P, width], F32, name="r")
-                    nc.scalar.activation(r[:], x[:], RELU)
-                    r_parts.append(r)
-                for part in range(parts):
-                    r, h_part = r_parts[part], h[:, part * width : (part + 1) * width]
+                    x_sb = work.tile([P, width], F32, name="x_sb")
                     if part < parts - 1:
-                        nc.scalar.activation(h_part, r[:], SQUARE)
+                        nc.scalar.activation(x_sb[:], x[:], RELU)
                     else:
-                        nc.vector.tensor_tensor(h_part, r[:], r[:], MULT)
+                        nc.scalar.copy(x_sb[:], x[:])
+                    moved.append(x_sb)
+                for part in range(parts):
+                    x_sb, h_part = moved[part], h[:, part * width : (part + 1) * width]
+                    if part < parts - 1:
+                        nc.scalar.activation(h_part, x_sb[:], SQUARE)
+                    else:
+                        nc.vector.scalar_tensor_tensor(h_part, x_sb[:], 0.0, x_sb[:], op0=MAX, op1=MULT)
                 h_tiles[piece, b] = h
 
         for store_first, store_last, widths in STORES:

@@ -12,7 +12,7 @@ PIECE = 512
 Q_BLOCKS = Q // P
 PSUM_BANKS = 8
 PIECES = N // PIECE
-STORES = ((0, 512, (384, 128)), (512, 768, (256,)), (768, 1024, (128, 128)))
+STORES = ((0, 512, (384, 128)), (512, 768, (256,)), (768, 1024, (192, 64)))
 
 FLOPS = 2 * P * Q * N + 2 * Q * P * N
 

@@ -79,9 +79,9 @@ def tile_gptmodel_kernel(tc, table, w, fc2, offs, out):
                         stop=(b == blocks[-1]),
                     )
                 copied = y_sb[:, first - store_first : first - store_first + width]
-                if piece == 0 or first + width == N:
-                    nc.scalar.copy(copied, y[:])
-                else:
+                if store_last == N and first + width < N:
                     nc.vector.tensor_copy(copied, y[:])
+                else:
+                    nc.scalar.copy(copied, y[:])
                 first += width
             nc.sync.dma_start(out[:, store_first:store_last], y_sb[:])

@@ -38,30 +38,31 @@ def tile_gptmodel_kernel(tc, table, w, fc2, offs, out):
         nc.sync.dma_start(fc2_sb[:], fc2.rearrange("(b p) d -> p b d", p=P))
 
         h_tiles = {}
-        for piece in range(PIECES):
-            for b in range(Q_BLOCKS):
-                parts = 2 if (piece, b) == (PIECES - 1, Q_BLOCKS - 1) else 1
-                width = PIECE // parts
-                h = hidden.tile([P, PIECE], BF16, name="h")
-                moved = []
-                for part in range(parts):
-                    first_id = piece * PIECE + part * width
-                    ids = offsets[:, first_id // 16 : (first_id + width) // 16]
-                    x = psum.tile([P, width], F32, name="x", tag="bank")
-                    nc.tensor.matmul(x[:], w_blocks[b], table_sb[:].indirect(ids), start=True, stop=True)
-                    x_sb = work.tile([P, width], F32, name="x_sb")
-                    if part < parts - 1:
-                        nc.scalar.activation(x_sb[:], x[:], RELU)
-                    else:
-                        nc.scalar.copy(x_sb[:], x[:])
-                    moved.append(x_sb)
-                for part in range(parts):
-                    x_sb, h_part = moved[part], h[:, part * width : (part + 1) * width]
-                    if part < parts - 1:
-                        nc.scalar.activation(h_part, x_sb[:], SQUARE)
-                    else:
-                        nc.vector.scalar_tensor_tensor(h_part, x_sb[:], 0.0, x_sb[:], op0=MAX, op1=MULT)
-                h_tiles[piece, b] = h
+        units = [(piece, 0) for piece in range(PIECES)]
+        units += [(piece, b) for piece in range(PIECES) for b in range(1, Q_BLOCKS)]
+        for piece, b in units:
+            parts = 2 if (piece, b) == (PIECES - 1, Q_BLOCKS - 1) else 1
+            width = PIECE // parts
+            h = hidden.tile([P, PIECE], BF16, name="h")
+            moved = []
+            for part in range(parts):
+                first_id = piece * PIECE + part * width
+                ids = offsets[:, first_id // 16 : (first_id + width) // 16]
+                x = psum.tile([P, width], F32, name="x", tag="bank")
+                nc.tensor.matmul(x[:], w_blocks[b], table_sb[:].indirect(ids), start=True, stop=True)
+                x_sb = work.tile([P, width], F32, name="x_sb")
+                if part < parts - 1:
+                    nc.scalar.activation(x_sb[:], x[:], RELU)
+                else:
+                    nc.scalar.copy(x_sb[:], x[:])
+                moved.append(x_sb)
+            for part in range(parts):
+                x_sb, h_part = moved[part], h[:, part * width : (part + 1) * width]
+                if part < parts - 1:
+                    nc.scalar.activation(h_part, x_sb[:], SQUARE)
+                else:
+                    nc.vector.scalar_tensor_tensor(h_part, x_sb[:], 0.0, x_sb[:], op0=MAX, op1=MULT)
+            h_tiles[piece, b] = h
 
         for store_first, store_last, widths in STORES:
             y_sb = work.tile([P, store_last - store_first], F32, name="y_sb")

import concourse.mybir as mybir

BF16, F32, U16 = mybir.dt.bfloat16, mybir.dt.float32, mybir.dt.uint16
RELU, SQUARE = mybir.ActivationFunctionType.Relu, mybir.ActivationFunctionType.Square
MAX, MULT = mybir.AluOpType.max, mybir.AluOpType.mult

P = 128
V = 4096
Q = 512
N = 1024
PIECE = 512
Q_BLOCKS = Q // P
PSUM_BANKS = 8
PIECES = N // PIECE
STORES = ((0, 512, (384, 128)), (512, 768, (256,)), (768, 1024, (192, 64)))

FLOPS = 2 * P * Q * N + 2 * Q * P * N


def tile_gptmodel_kernel(tc, table, w, fc2, offs, out):
    nc = tc.nc
    with (
        tc.tile_pool(name="held", bufs=1) as held,
        tc.tile_pool(name="work", bufs=4) as work,
        tc.tile_pool(name="hidden", bufs=PIECES * Q_BLOCKS) as hidden,
        tc.psum_pool(name="psum", bufs=PSUM_BANKS) as psum,
    ):
        table_sb = held.tile([P, V], BF16, name="table_sb")
        nc.sync.dma_start(table_sb[:], table)
        offsets = held.tile([P, N // 16], U16, name="offsets")
        nc.sync.dma_start(offsets[:], offs)
        w_first = held.tile([P, P], BF16, name="w_first")
        nc.sync.dma_start(w_first[:], w[:, 0:P])
        w_rest = held.tile([P, Q - P], BF16, name="w_rest")
        nc.sync.dma_start(w_rest[:], w[:, P:Q])
        w_blocks = [w_first[:]] + [w_rest[:, (b - 1) * P : b * P] for b in range(1, Q_BLOCKS)]
        fc2_sb = held.tile([P, Q_BLOCKS, P], BF16, name="fc2_sb")
        nc.sync.dma_start(fc2_sb[:], fc2.rearrange("(b p) d -> p b d", p=P))

        h_tiles = {}
        units = [(piece, 0) for piece in range(PIECES)]
        units += [(piece, b) for piece in range(PIECES) for b in range(1, Q_BLOCKS)]
        for piece, b in units:
            parts = 2 if (piece, b) == (PIECES - 1, Q_BLOCKS - 1) else 1
            width = PIECE // parts
            h = hidden.tile([P, PIECE], BF16, name="h")
            moved = []
            for part in range(parts):
                first_id = piece * PIECE + part * width
                ids = offsets[:, first_id // 16 : (first_id + width) // 16]
                x = psum.tile([P, width], F32, name="x", tag="bank")
                nc.tensor.matmul(x[:], w_blocks[b], table_sb[:].indirect(ids), start=True, stop=True)
                x_sb = work.tile([P, width], F32, name="x_sb")
                if part < parts - 1:
                    nc.scalar.activation(x_sb[:], x[:], RELU)
                else:
                    nc.scalar.copy(x_sb[:], x[:])
                moved.append(x_sb)
            for part in range(parts):
                x_sb, h_part = moved[part], h[:, part * width : (part + 1) * width]
                if part < parts - 1:
                    nc.scalar.activation(h_part, x_sb[:], SQUARE)
                else:
                    nc.vector.scalar_tensor_tensor(h_part, x_sb[:], 0.0, x_sb[:], op0=MAX, op1=MULT)
            h_tiles[piece, b] = h

        for store_first, store_last, widths in STORES:
            y_sb = work.tile([P, store_last - store_first], F32, name="y_sb")
            first = store_first
            for width in widths:
                piece, column = first // PIECE, first % PIECE
                y = psum.tile([P, width], F32, name="y", tag="bank")
                blocks = list(range(Q_BLOCKS)) if column == 0 else [Q_BLOCKS - 1] + list(range(Q_BLOCKS - 1))
                for b in blocks:
                    nc.tensor.matmul(
                        y[:],
                        fc2_sb[:, b, :],
                        h_tiles[piece, b][:, column : column + width],
                        start=(b == blocks[0]),
                        stop=(b == blocks[-1]),
                    )
                copied = y_sb[:, first - store_first : first - store_first + width]
                if store_last == N and first + width < N:
                    nc.vector.tensor_copy(copied, y[:])
                else:
                    nc.scalar.copy(copied, y[:])
                first += width
            nc.sync.dma_start(out[:, store_first:store_last], y_sb[:])
